import numpy as np
import ml_dtypes

BF16 = ml_dtypes.bfloat16


def bf(x):
    return np.asarray(x, np.float32).astype(BF16)


def f32(x):
    return np.asarray(x, np.float32)


def f64(x):
    return np.asarray(x).astype(np.float64)


def striped(idx):
    return np.tile(idx.reshape(-1, 16).T, (8, 1))


C, S, N, D = 512, 512, 128, 256


def setup_inputs():
    return {"base": f32(4.0 + np.random.standard_normal((C, S))), "x": bf(np.random.standard_normal((D, N)) * np.sqrt(2.0 / D)), "cent": bf(np.random.standard_normal((D, C)) * np.sqrt(2.0 / D)), "offs": striped(np.random.permutation(S)[:N])}


def reference(base, x, cent, offs):
    idx = offs[:16].T.reshape(-1)
    xv = f64(x)
    cv = f64(cent)
    xsq = np.sum(xv * xv, axis=0)[None, :]
    csq = np.sum(cv * cv, axis=0)[:, None]
    cross = cv.T @ xv
    out = f64(base).copy()
    out[:, idx] = (xsq + csq) + (-2.0 * cross)
    return out

@@ -1,0 +1,64 @@
+import concourse.mybir as mybir
+
+BF16, F32, U16 = mybir.dt.bfloat16, mybir.dt.float32, mybir.dt.uint16
+ADD, MULT = mybir.AluOpType.add, mybir.AluOpType.mult
+COPY = mybir.ActivationFunctionType.Copy
+
+P = 128
+C, S, N, D = 512, 512, 128, 256
+C_BLOCKS = C // P
+D_BLOCKS = D // P
+
+FLOPS = 2 * C * N * D + 2 * D * (C + N) + 3 * C * N
+
+
+def tile_geometricactivation_kernel(tc, base, x, cent, offs, out):
+    nc = tc.nc
+    with (
+        tc.tile_pool(name="held", bufs=1) as held,
+        tc.tile_pool(name="windows", bufs=C_BLOCKS) as windows,
+        tc.tile_pool(name="terms", bufs=2) as terms,
+        tc.psum_pool(name="psum", bufs=2) as psum,
+    ):
+        offsets = held.tile([P, N // 16], U16, name="offsets")
+        nc.sync.dma_start(offsets[:], offs)
+
+        x_sb = held.tile([P, D_BLOCKS, N], BF16, name="x_sb")
+        nc.sync.dma_start(x_sb[:], x.rearrange("(k p) j -> p k j", p=P))
+        cent_sb = held.tile([P, D_BLOCKS, C], BF16, name="cent_sb")
+        nc.scalar.dma_start(cent_sb[:], cent.rearrange("(k p) c -> p k c", p=P))
+
+        ones = held.tile([P, P], BF16, name="ones")
+        nc.vector.memset(ones[:], 1.0)
+        x_squares = held.tile([P, D_BLOCKS, N], BF16, name="x_squares")
+        nc.vector.tensor_tensor(x_squares[:], x_sb[:], x_sb[:], MULT)
+        cent_squares = held.tile([P, D_BLOCKS, C], BF16, name="cent_squares")
+        nc.vector.tensor_tensor(cent_squares[:], cent_sb[:], cent_sb[:], MULT)
+
+        for cb in range(C_BLOCKS):
+            rows = slice(cb * P, (cb + 1) * P)
+
+            window = windows.tile([P, S], F32, name="window")
+            nc.sync.dma_start(window[:], base[rows, :])
+
+            cross_ps = psum.tile([P, N], F32, name="cross_ps")
+            for k in range(D_BLOCKS):
+                nc.tensor.matmul(
+                    cross_ps[:], cent_sb[:, k, rows], x_sb[:, k, :], start=(k == 0), stop=(k == D_BLOCKS - 1)
+                )
+
+            norms_ps = psum.tile([P, N], F32, name="norms_ps")
+            for k in range(D_BLOCKS):
+                nc.tensor.matmul(norms_ps[:], ones[:], x_squares[:, k, :], start=(k == 0), stop=False)
+            for k in range(D_BLOCKS):
+                nc.tensor.matmul(
+                    norms_ps[:], cent_squares[:, k, rows], ones[:], start=False, stop=(k == D_BLOCKS - 1)
+                )
+
+            norms_term = terms.tile([P, N], F32, name="norms_term")
+            nc.scalar.activation(norms_term[:], norms_ps[:], COPY)
+            cross_term = terms.tile([P, N], F32, name="cross_term")
+            nc.scalar.activation(cross_term[:], cross_ps[:], COPY, scale=-2.0)
+
+            nc.vector.tensor_tensor(window[:].indirect(offsets[:]), norms_term[:], cross_term[:], ADD)
+            nc.sync.dma_start(out[rows, :], window[:])

@@ -20,13 +20,21 @@ def tile_geometricactivation_kernel(tc, base, x, cent, offs, out):
         tc.tile_pool(name="terms", bufs=2) as terms,
         tc.psum_pool(name="psum", bufs=2) as psum,
     ):
-        offsets = held.tile([P, N // 16], U16, name="offsets")
-        nc.sync.dma_start(offsets[:], offs)
-
         x_sb = held.tile([P, D_BLOCKS, N], BF16, name="x_sb")
         nc.sync.dma_start(x_sb[:], x.rearrange("(k p) j -> p k j", p=P))
         cent_sb = held.tile([P, D_BLOCKS, C], BF16, name="cent_sb")
-        nc.scalar.dma_start(cent_sb[:], cent.rearrange("(k p) c -> p k c", p=P))
+        for k, queue in enumerate((nc.scalar, nc.sync)):
+            queue.dma_start(cent_sb[:, k, :], cent[k * P : (k + 1) * P, :])
+
+        offsets = held.tile([P, N // 16], U16, name="offsets")
+        nc.sync.dma_start(offsets[:], offs)
+
+        window_of = []
+        for cb in range(C_BLOCKS):
+            window = windows.tile([P, S], F32, name="window")
+            queue = nc.scalar if cb % 2 == 0 else nc.sync
+            queue.dma_start(window[:], base[cb * P : (cb + 1) * P, :])
+            window_of.append(window)
 
         ones = held.tile([P, P], BF16, name="ones")
         nc.vector.memset(ones[:], 1.0)
@@ -37,9 +45,7 @@ def tile_geometricactivation_kernel(tc, base, x, cent, offs, out):
 
         for cb in range(C_BLOCKS):
             rows = slice(cb * P, (cb + 1) * P)
-
-            window = windows.tile([P, S], F32, name="window")
-            nc.sync.dma_start(window[:], base[rows, :])
+            window = window_of[cb]
 
             cross_ps = psum.tile([P, N], F32, name="cross_ps")
             for k in range(D_BLOCKS):

@@ -41,7 +41,9 @@ def tile_geometricactivation_kernel(tc, base, x, cent, offs, out):
         x_squares = held.tile([P, D_BLOCKS, N], BF16, name="x_squares")
         nc.vector.tensor_tensor(x_squares[:], x_sb[:], x_sb[:], MULT)
         cent_squares = held.tile([P, D_BLOCKS, C], BF16, name="cent_squares")
-        nc.vector.tensor_tensor(cent_squares[:], cent_sb[:], cent_sb[:], MULT)
+        for cb in range(C_BLOCKS):
+            rows = slice(cb * P, (cb + 1) * P)
+            nc.vector.tensor_tensor(cent_squares[:, :, rows], cent_sb[:, :, rows], cent_sb[:, :, rows], MULT)
 
         for cb in range(C_BLOCKS):
             rows = slice(cb * P, (cb + 1) * P)
@@ -52,6 +54,8 @@ def tile_geometricactivation_kernel(tc, base, x, cent, offs, out):
                 nc.tensor.matmul(
                     cross_ps[:], cent_sb[:, k, rows], x_sb[:, k, :], start=(k == 0), stop=(k == D_BLOCKS - 1)
                 )
+            cross_term = terms.tile([P, N], F32, name="cross_term")
+            nc.scalar.activation(cross_term[:], cross_ps[:], COPY, scale=-2.0)
 
             norms_ps = psum.tile([P, N], F32, name="norms_ps")
             for k in range(D_BLOCKS):
@@ -63,8 +67,6 @@ def tile_geometricactivation_kernel(tc, base, x, cent, offs, out):
 
             norms_term = terms.tile([P, N], F32, name="norms_term")
             nc.scalar.activation(norms_term[:], norms_ps[:], COPY)
-            cross_term = terms.tile([P, N], F32, name="cross_term")
-            nc.scalar.activation(cross_term[:], cross_ps[:], COPY, scale=-2.0)
 
             nc.vector.tensor_tensor(window[:].indirect(offsets[:]), norms_term[:], cross_term[:], ADD)
             nc.sync.dma_start(out[rows, :], window[:])

@@ -8,6 +8,8 @@ P = 128
 C, S, N, D = 512, 512, 128, 256
 C_BLOCKS = C // P
 D_BLOCKS = D // P
+BANK = 512
+WARM_MATMULS = 4
 
 FLOPS = 2 * C * N * D + 2 * D * (C + N) + 3 * C * N
 
@@ -19,6 +21,7 @@ def tile_geometricactivation_kernel(tc, base, x, cent, offs, out):
         tc.tile_pool(name="windows", bufs=C_BLOCKS) as windows,
         tc.tile_pool(name="terms", bufs=2) as terms,
         tc.psum_pool(name="psum", bufs=2) as psum,
+        tc.psum_pool(name="warm", bufs=1) as warm,
     ):
         x_sb = held.tile([P, D_BLOCKS, N], BF16, name="x_sb")
         nc.sync.dma_start(x_sb[:], x.rearrange("(k p) j -> p k j", p=P))
@@ -38,6 +41,13 @@ def tile_geometricactivation_kernel(tc, base, x, cent, offs, out):
 
         ones = held.tile([P, P], BF16, name="ones")
         nc.vector.memset(ones[:], 1.0)
+
+        many_ones = held.tile([P, BANK], BF16, name="many_ones")
+        nc.vector.memset(many_ones[:], 1.0)
+        warm_ps = warm.tile([P, BANK], F32, name="warm_ps")
+        for w in range(WARM_MATMULS):
+            nc.tensor.matmul(warm_ps[:], ones[:], many_ones[:], start=True, stop=True)
+
         x_squares = held.tile([P, D_BLOCKS, N], BF16, name="x_squares")
         nc.vector.tensor_tensor(x_squares[:], x_sb[:], x_sb[:], MULT)
         cent_squares = held.tile([P, D_BLOCKS, C], BF16, name="cent_squares")

@@ -26,8 +26,8 @@ def tile_geometricactivation_kernel(tc, base, x, cent, offs, out):
         x_sb = held.tile([P, D_BLOCKS, N], BF16, name="x_sb")
         nc.sync.dma_start(x_sb[:], x.rearrange("(k p) j -> p k j", p=P))
         cent_sb = held.tile([P, D_BLOCKS, C], BF16, name="cent_sb")
-        for k, queue in enumerate((nc.scalar, nc.sync)):
-            queue.dma_start(cent_sb[:, k, :], cent[k * P : (k + 1) * P, :])
+        for k in range(D_BLOCKS):
+            nc.sync.dma_start(cent_sb[:, k, :], cent[k * P : (k + 1) * P, :])
 
         offsets = held.tile([P, N // 16], U16, name="offsets")
         nc.sync.dma_start(offsets[:], offs)
@@ -35,8 +35,7 @@ def tile_geometricactivation_kernel(tc, base, x, cent, offs, out):
         window_of = []
         for cb in range(C_BLOCKS):
             window = windows.tile([P, S], F32, name="window")
-            queue = nc.scalar if cb % 2 == 0 else nc.sync
-            queue.dma_start(window[:], base[cb * P : (cb + 1) * P, :])
+            nc.sync.dma_start(window[:], base[cb * P : (cb + 1) * P, :])
             window_of.append(window)
 
         ones = held.tile([P, P], BF16, name="ones")

@@ -8,8 +8,7 @@ P = 128
 C, S, N, D = 512, 512, 128, 256
 C_BLOCKS = C // P
 D_BLOCKS = D // P
-BANK = 512
-WARM_MATMULS = 4
+WARM_MATMULS = 16
 
 FLOPS = 2 * C * N * D + 2 * D * (C + N) + 3 * C * N
 
@@ -41,11 +40,9 @@ def tile_geometricactivation_kernel(tc, base, x, cent, offs, out):
         ones = held.tile([P, P], BF16, name="ones")
         nc.vector.memset(ones[:], 1.0)
 
-        many_ones = held.tile([P, BANK], BF16, name="many_ones")
-        nc.vector.memset(many_ones[:], 1.0)
-        warm_ps = warm.tile([P, BANK], F32, name="warm_ps")
+        warm_ps = warm.tile([P, P], F32, name="warm_ps")
         for w in range(WARM_MATMULS):
-            nc.tensor.matmul(warm_ps[:], ones[:], many_ones[:], start=True, stop=True)
+            nc.tensor.matmul(warm_ps[:], ones[:], ones[:], start=True, stop=True)
 
         x_squares = held.tile([P, D_BLOCKS, N], BF16, name="x_squares")
         nc.vector.tensor_tensor(x_squares[:], x_sb[:], x_sb[:], MULT)

@@ -18,7 +18,7 @@ def tile_geometricactivation_kernel(tc, base, x, cent, offs, out):
     with (
         tc.tile_pool(name="held", bufs=1) as held,
         tc.tile_pool(name="windows", bufs=C_BLOCKS) as windows,
-        tc.tile_pool(name="terms", bufs=2) as terms,
+        tc.tile_pool(name="terms", bufs=C_BLOCKS) as terms,
         tc.psum_pool(name="psum", bufs=2) as psum,
         tc.psum_pool(name="warm", bufs=1) as warm,
     ):

@@ -8,7 +8,7 @@ P = 128
 C, S, N, D = 512, 512, 128, 256
 C_BLOCKS = C // P
 D_BLOCKS = D // P
-WARM_MATMULS = 16
+WARM_MATMULS = 12
 
 FLOPS = 2 * C * N * D + 2 * D * (C + N) + 3 * C * N
 

@@ -23,19 +23,24 @@ def tile_geometricactivation_kernel(tc, base, x, cent, offs, out):
         tc.psum_pool(name="warm", bufs=1) as warm,
     ):
         x_sb = held.tile([P, D_BLOCKS, N], BF16, name="x_sb")
-        nc.sync.dma_start(x_sb[:], x.rearrange("(k p) j -> p k j", p=P))
-        cent_sb = held.tile([P, D_BLOCKS, C], BF16, name="cent_sb")
-        for k in range(D_BLOCKS):
-            nc.sync.dma_start(cent_sb[:, k, :], cent[k * P : (k + 1) * P, :])
+        nc.sync.dma_start(x_sb[:], x.rearrange("(p k) j -> p k j", k=D_BLOCKS))
+        cent_rows = cent.rearrange("(p k) c -> p k c", k=D_BLOCKS)
+        half = C // 2
+        cent_low = held.tile([P, D_BLOCKS, half], BF16, name="cent_low")
+        nc.sync.dma_start(cent_low[:], cent_rows[:, :, :half])
 
         offsets = held.tile([P, N // 16], U16, name="offsets")
         nc.sync.dma_start(offsets[:], offs)
 
         window_of = []
+        cent_high = held.tile([P, D_BLOCKS, half], BF16, name="cent_high")
         for cb in range(C_BLOCKS):
             window = windows.tile([P, S], F32, name="window")
             nc.sync.dma_start(window[:], base[cb * P : (cb + 1) * P, :])
             window_of.append(window)
+            if cb == 0:
+                nc.sync.dma_start(cent_high[:], cent_rows[:, :, half:])
+        cent_of = [cent_half[:, :, b * P : (b + 1) * P] for cent_half in (cent_low, cent_high) for b in range(2)]
 
         ones = held.tile([P, P], BF16, name="ones")
         nc.vector.memset(ones[:], 1.0)
@@ -46,10 +51,11 @@ def tile_geometricactivation_kernel(tc, base, x, cent, offs, out):
 
         x_squares = held.tile([P, D_BLOCKS, N], BF16, name="x_squares")
         nc.vector.tensor_tensor(x_squares[:], x_sb[:], x_sb[:], MULT)
-        cent_squares = held.tile([P, D_BLOCKS, C], BF16, name="cent_squares")
+        squares_of = []
         for cb in range(C_BLOCKS):
-            rows = slice(cb * P, (cb + 1) * P)
-            nc.vector.tensor_tensor(cent_squares[:, :, rows], cent_sb[:, :, rows], cent_sb[:, :, rows], MULT)
+            cent_squares = held.tile([P, D_BLOCKS, P], BF16, name=f"cent_squares{cb}")
+            nc.vector.tensor_tensor(cent_squares[:], cent_of[cb], cent_of[cb], MULT)
+            squares_of.append(cent_squares)
 
         for cb in range(C_BLOCKS):
             rows = slice(cb * P, (cb + 1) * P)
@@ -58,18 +64,16 @@ def tile_geometricactivation_kernel(tc, base, x, cent, offs, out):
             cross_ps = psum.tile([P, N], F32, name="cross_ps")
             for k in range(D_BLOCKS):
                 nc.tensor.matmul(
-                    cross_ps[:], cent_sb[:, k, rows], x_sb[:, k, :], start=(k == 0), stop=(k == D_BLOCKS - 1)
+                    cross_ps[:], cent_of[cb][:, k, :], x_sb[:, k, :], start=(k == 0), stop=(k == D_BLOCKS - 1)
                 )
             cross_term = terms.tile([P, N], F32, name="cross_term")
             nc.scalar.activation(cross_term[:], cross_ps[:], COPY, scale=-2.0)
 
             norms_ps = psum.tile([P, N], F32, name="norms_ps")
             for k in range(D_BLOCKS):
-                nc.tensor.matmul(norms_ps[:], ones[:], x_squares[:, k, :], start=(k == 0), stop=False)
+                nc.tensor.matmul(norms_ps[:], squares_of[cb][:, k, :], ones[:], start=(k == 0), stop=False)
             for k in range(D_BLOCKS):
-                nc.tensor.matmul(
-                    norms_ps[:], cent_squares[:, k, rows], ones[:], start=False, stop=(k == D_BLOCKS - 1)
-                )
+                nc.tensor.matmul(norms_ps[:], ones[:], x_squares[:, k, :], start=False, stop=(k == D_BLOCKS - 1))
 
             norms_term = terms.tile([P, N], F32, name="norms_term")
             nc.scalar.activation(norms_term[:], norms_ps[:], COPY)

@@ -17,7 +17,7 @@ def tile_geometricactivation_kernel(tc, base, x, cent, offs, out):
     nc = tc.nc
     with (
         tc.tile_pool(name="held", bufs=1) as held,
-        tc.tile_pool(name="windows", bufs=C_BLOCKS) as windows,
+        tc.tile_pool(name="windows", bufs=1) as windows,
         tc.tile_pool(name="terms", bufs=C_BLOCKS) as terms,
         tc.psum_pool(name="psum", bufs=2) as psum,
         tc.psum_pool(name="warm", bufs=1) as warm,
@@ -25,22 +25,21 @@ def tile_geometricactivation_kernel(tc, base, x, cent, offs, out):
         x_sb = held.tile([P, D_BLOCKS, N], BF16, name="x_sb")
         nc.sync.dma_start(x_sb[:], x.rearrange("(p k) j -> p k j", k=D_BLOCKS))
         cent_rows = cent.rearrange("(p k) c -> p k c", k=D_BLOCKS)
-        half = C // 2
-        cent_low = held.tile([P, D_BLOCKS, half], BF16, name="cent_low")
-        nc.sync.dma_start(cent_low[:], cent_rows[:, :, :half])
+        cent_0 = held.tile([P, D_BLOCKS, P], BF16, name="cent_0")
+        nc.sync.dma_start(cent_0[:], cent_rows[:, :, :P])
 
         offsets = held.tile([P, N // 16], U16, name="offsets")
         nc.sync.dma_start(offsets[:], offs)
 
-        window_of = []
-        cent_high = held.tile([P, D_BLOCKS, half], BF16, name="cent_high")
-        for cb in range(C_BLOCKS):
-            window = windows.tile([P, S], F32, name="window")
-            nc.sync.dma_start(window[:], base[cb * P : (cb + 1) * P, :])
-            window_of.append(window)
-            if cb == 0:
-                nc.sync.dma_start(cent_high[:], cent_rows[:, :, half:])
-        cent_of = [cent_half[:, :, b * P : (b + 1) * P] for cent_half in (cent_low, cent_high) for b in range(2)]
+        window_of = [windows.tile([P, S], F32, name=f"window{cb}") for cb in range(C_BLOCKS)]
+        nc.sync.dma_start(window_of[0][:], base[:P, :])
+        cent_1 = held.tile([P, D_BLOCKS, P], BF16, name="cent_1")
+        nc.sync.dma_start(cent_1[:], cent_rows[:, :, P : 2 * P])
+        cent_high = held.tile([P, D_BLOCKS, 2 * P], BF16, name="cent_high")
+        nc.sync.dma_start(cent_high[:], cent_rows[:, :, 2 * P :])
+        for cb in range(1, C_BLOCKS):
+            nc.sync.dma_start(window_of[cb][:], base[cb * P : (cb + 1) * P, :])
+        cent_of = [cent_0[:], cent_1[:], cent_high[:, :, :P], cent_high[:, :, P:]]
 
         ones = held.tile([P, P], BF16, name="ones")
         nc.vector.memset(ones[:], 1.0)

@@ -17,7 +17,7 @@ def tile_geometricactivation_kernel(tc, base, x, cent, offs, out):
     nc = tc.nc
     with (
         tc.tile_pool(name="held", bufs=1) as held,
-        tc.tile_pool(name="windows", bufs=1) as windows,
+        tc.tile_pool(name="windows", bufs=C_BLOCKS) as windows,
         tc.tile_pool(name="terms", bufs=C_BLOCKS) as terms,
         tc.psum_pool(name="psum", bufs=2) as psum,
         tc.psum_pool(name="warm", bufs=1) as warm,
@@ -27,18 +27,19 @@ def tile_geometricactivation_kernel(tc, base, x, cent, offs, out):
         cent_rows = cent.rearrange("(p k) c -> p k c", k=D_BLOCKS)
         cent_0 = held.tile([P, D_BLOCKS, P], BF16, name="cent_0")
         nc.sync.dma_start(cent_0[:], cent_rows[:, :, :P])
-
-        offsets = held.tile([P, N // 16], U16, name="offsets")
-        nc.sync.dma_start(offsets[:], offs)
-
-        window_of = [windows.tile([P, S], F32, name=f"window{cb}") for cb in range(C_BLOCKS)]
-        nc.sync.dma_start(window_of[0][:], base[:P, :])
         cent_1 = held.tile([P, D_BLOCKS, P], BF16, name="cent_1")
         nc.sync.dma_start(cent_1[:], cent_rows[:, :, P : 2 * P])
         cent_high = held.tile([P, D_BLOCKS, 2 * P], BF16, name="cent_high")
         nc.sync.dma_start(cent_high[:], cent_rows[:, :, 2 * P :])
-        for cb in range(1, C_BLOCKS):
-            nc.sync.dma_start(window_of[cb][:], base[cb * P : (cb + 1) * P, :])
+
+        offsets = held.tile([P, N // 16], U16, name="offsets")
+        nc.sync.dma_start(offsets[:], offs)
+
+        window_of = []
+        for cb in range(C_BLOCKS):
+            window = windows.tile([P, S], F32, name="window")
+            nc.sync.dma_start(window[:], base[cb * P : (cb + 1) * P, :])
+            window_of.append(window)
         cent_of = [cent_0[:], cent_1[:], cent_high[:, :, :P], cent_high[:, :, P:]]
 
         ones = held.tile([P, P], BF16, name="ones")

@@ -27,10 +27,8 @@ def tile_geometricactivation_kernel(tc, base, x, cent, offs, out):
         cent_rows = cent.rearrange("(p k) c -> p k c", k=D_BLOCKS)
         cent_0 = held.tile([P, D_BLOCKS, P], BF16, name="cent_0")
         nc.sync.dma_start(cent_0[:], cent_rows[:, :, :P])
-        cent_1 = held.tile([P, D_BLOCKS, P], BF16, name="cent_1")
-        nc.sync.dma_start(cent_1[:], cent_rows[:, :, P : 2 * P])
-        cent_high = held.tile([P, D_BLOCKS, 2 * P], BF16, name="cent_high")
-        nc.sync.dma_start(cent_high[:], cent_rows[:, :, 2 * P :])
+        cent_rest = held.tile([P, D_BLOCKS, C - P], BF16, name="cent_rest")
+        nc.sync.dma_start(cent_rest[:], cent_rows[:, :, P:])
 
         offsets = held.tile([P, N // 16], U16, name="offsets")
         nc.sync.dma_start(offsets[:], offs)
@@ -40,7 +38,7 @@ def tile_geometricactivation_kernel(tc, base, x, cent, offs, out):
             window = windows.tile([P, S], F32, name="window")
             nc.sync.dma_start(window[:], base[cb * P : (cb + 1) * P, :])
             window_of.append(window)
-        cent_of = [cent_0[:], cent_1[:], cent_high[:, :, :P], cent_high[:, :, P:]]
+        cent_of = [cent_0[:]] + [cent_rest[:, :, b * P : (b + 1) * P] for b in range(C_BLOCKS - 1)]
 
         ones = held.tile([P, P], BF16, name="ones")
         nc.vector.memset(ones[:], 1.0)

import concourse.mybir as mybir

BF16, F32, U16 = mybir.dt.bfloat16, mybir.dt.float32, mybir.dt.uint16
ADD, MULT = mybir.AluOpType.add, mybir.AluOpType.mult
COPY = mybir.ActivationFunctionType.Copy

P = 128
C, S, N, D = 512, 512, 128, 256
C_BLOCKS = C // P
D_BLOCKS = D // P
WARM_MATMULS = 12

FLOPS = 2 * C * N * D + 2 * D * (C + N) + 3 * C * N


def tile_geometricactivation_kernel(tc, base, x, cent, offs, out):
    nc = tc.nc
    with (
        tc.tile_pool(name="held", bufs=1) as held,
        tc.tile_pool(name="windows", bufs=C_BLOCKS) as windows,
        tc.tile_pool(name="terms", bufs=C_BLOCKS) as terms,
        tc.psum_pool(name="psum", bufs=2) as psum,
        tc.psum_pool(name="warm", bufs=1) as warm,
    ):
        x_sb = held.tile([P, D_BLOCKS, N], BF16, name="x_sb")
        nc.sync.dma_start(x_sb[:], x.rearrange("(p k) j -> p k j", k=D_BLOCKS))
        cent_rows = cent.rearrange("(p k) c -> p k c", k=D_BLOCKS)
        cent_0 = held.tile([P, D_BLOCKS, P], BF16, name="cent_0")
        nc.sync.dma_start(cent_0[:], cent_rows[:, :, :P])
        cent_rest = held.tile([P, D_BLOCKS, C - P], BF16, name="cent_rest")
        nc.sync.dma_start(cent_rest[:], cent_rows[:, :, P:])

        offsets = held.tile([P, N // 16], U16, name="offsets")
        nc.sync.dma_start(offsets[:], offs)

        window_of = []
        for cb in range(C_BLOCKS):
            window = windows.tile([P, S], F32, name="window")
            nc.sync.dma_start(window[:], base[cb * P : (cb + 1) * P, :])
            window_of.append(window)
        cent_of = [cent_0[:]] + [cent_rest[:, :, b * P : (b + 1) * P] for b in range(C_BLOCKS - 1)]

        ones = held.tile([P, P], BF16, name="ones")
        nc.vector.memset(ones[:], 1.0)

        warm_ps = warm.tile([P, P], F32, name="warm_ps")
        for w in range(WARM_MATMULS):
            nc.tensor.matmul(warm_ps[:], ones[:], ones[:], start=True, stop=True)

        x_squares = held.tile([P, D_BLOCKS, N], BF16, name="x_squares")
        nc.vector.tensor_tensor(x_squares[:], x_sb[:], x_sb[:], MULT)
        squares_of = []
        for cb in range(C_BLOCKS):
            cent_squares = held.tile([P, D_BLOCKS, P], BF16, name=f"cent_squares{cb}")
            nc.vector.tensor_tensor(cent_squares[:], cent_of[cb], cent_of[cb], MULT)
            squares_of.append(cent_squares)

        for cb in range(C_BLOCKS):
            rows = slice(cb * P, (cb + 1) * P)
            window = window_of[cb]

            cross_ps = psum.tile([P, N], F32, name="cross_ps")
            for k in range(D_BLOCKS):
                nc.tensor.matmul(
                    cross_ps[:], cent_of[cb][:, k, :], x_sb[:, k, :], start=(k == 0), stop=(k == D_BLOCKS - 1)
                )
            cross_term = terms.tile([P, N], F32, name="cross_term")
            nc.scalar.activation(cross_term[:], cross_ps[:], COPY, scale=-2.0)

            norms_ps = psum.tile([P, N], F32, name="norms_ps")
            for k in range(D_BLOCKS):
                nc.tensor.matmul(norms_ps[:], squares_of[cb][:, k, :], ones[:], start=(k == 0), stop=False)
            for k in range(D_BLOCKS):
                nc.tensor.matmul(norms_ps[:], ones[:], x_squares[:, k, :], start=False, stop=(k == D_BLOCKS - 1))

            norms_term = terms.tile([P, N], F32, name="norms_term")
            nc.scalar.activation(norms_term[:], norms_ps[:], COPY)

            nc.vector.tensor_tensor(window[:].indirect(offsets[:]), norms_term[:], cross_term[:], ADD)
            nc.sync.dma_start(out[rows, :], window[:])
